import numpy as np
import ml_dtypes


def mxq(x, axis, fmt="e4m3"):
    dtype, down = {"e4m3": (ml_dtypes.float8_e4m3fn, 7), "e5m2": (ml_dtypes.float8_e5m2, 14)}[fmt]
    v = np.moveaxis(np.asarray(x, np.float32).astype(ml_dtypes.bfloat16).astype(np.float64), axis, -1)
    blocks = v.reshape(v.shape[:-1] + (-1, 32))
    amax = np.abs(blocks).max(-1, keepdims=True)
    byte = np.maximum(np.where(amax > 0, np.frexp(amax)[1] - 1 + 127, 0) - down, 1)
    scale = np.exp2(byte - 127.0)
    codes = (blocks / scale).astype(np.float32).astype(dtype).astype(np.float64)
    return np.moveaxis((codes * scale).reshape(v.shape), -1, axis)


WIDE = False


def mx_kscale(k):
    if not WIDE:
        return np.ones(k)
    levels = np.array([10, -10, 5, -5, 0])
    a = np.random.permutation(np.resize(levels, k // 512 * 4)).reshape(k // 512, 4)
    idx = np.arange(k)
    return np.exp2(a[idx // 512, idx % 128 // 32])


BF16 = ml_dtypes.bfloat16


def bf(x):
    return np.asarray(x, np.float32).astype(BF16)


def f64(x):
    return np.asarray(x).astype(np.float64)


T, D, F, R = 4096, 512, 512, 128


def silu(v):
    return v / (1.0 + np.exp(-v))


def setup_inputs():
    s = mx_kscale(D)
    return {
        "x": bf(np.random.standard_normal((T, D)) * s),
        "xa": bf(np.random.standard_normal((T, R))),
        "W_gate_up": bf(np.random.standard_normal((D, 2 * F)) / np.sqrt(D) / s[:, None]),
        "B_gate_up": bf(np.random.standard_normal((R, 2 * F)) * 0.5 / np.sqrt(R)),
        "A_down": bf(np.random.standard_normal((F, R)) / np.sqrt(F)),
    }


def reference(x, xa, W_gate_up, B_gate_up, A_down):
    gate_up = (mxq(f64(x), 1, "e4m3") @ mxq(f64(W_gate_up), 0, "e4m3")) + f64(xa) @ f64(B_gate_up)
    gate, up = gate_up[:, :F], gate_up[:, F:]
    h = silu(gate) * up
    ha = mxq(h, 1, "e4m3") @ mxq(f64(A_down), 0, "e4m3")
    return h, ha

@@ -1,0 +1,330 @@
+from contextlib import ExitStack
+
+import concourse.bass as bass
+import concourse.mybir as mybir
+import concourse.tile as tile
+from concourse.masks import make_identity
+
+F32 = mybir.dt.float32
+BF16 = mybir.dt.bfloat16
+U32 = mybir.dt.uint32
+U8 = mybir.dt.uint8
+FP8X4 = mybir.dt.float8_e4m3fn_x4
+ADD = mybir.AluOpType.add
+MULT = mybir.AluOpType.mult
+SILU = mybir.ActivationFunctionType.Silu
+
+T, D, F, R = 4096, 512, 512, 128
+P = 128
+NT = T // P
+NP = NT // 2
+FLOPS = 2 * T * D * 2 * F + 2 * T * R * 2 * F + 2 * T * F * R
+
+PIN = False
+LX = 2
+LH = 2
+LL = 4
+LL0 = 2
+XCH = 4
+LS_BUFS = 12
+TAIL_S = 2
+HT2S = 0
+HA_ENG = "S"
+
+
+def tile_loramlp_pa_t_kernel(tc, x, xa, W_gate_up, B_gate_up, A_down, out_0, out_1):
+    nc = tc.nc
+    with ExitStack() as ctx:
+        const = ctx.enter_context(tc.tile_pool(name="const", bufs=1))
+        work = ctx.enter_context(tc.tile_pool(name="work", bufs=3))
+        ps = ctx.enter_context(tc.psum_pool(name="ps", bufs=8))
+        if PIN:
+            ctx.enter_context(tc.manual_schedule())
+
+        x_v = x.rearrange("(p i) d -> p i d", i=NT)
+        xa_v = xa.rearrange("(p i) r -> p i r", i=NT)
+        h_v = out_0.rearrange("(p i) f -> p i f", i=NT)
+        ha_v = out_1.rearrange("(p i) r -> p i r", i=NT)
+
+        zero = const.tile([P, 1], F32, name="zero")
+        warm = const.tile([P, 1], F32, name="warm")
+        nc.vector.memset(zero[:], 0.0)
+        nc.scalar.activation(out=warm[:], in_=zero[:], func=SILU)
+        ident_b = const.tile([P, P], BF16, name="ident_b")
+        make_identity(nc, ident_b[:])
+        ident_f = const.tile([P, P], F32, name="ident_f")
+        make_identity(nc, ident_f[:])
+
+        xa_sb = [const.tile([P, 8 * R], BF16, name="xa_sb%d" % c) for c in range(4)]
+        x_sb = [const.tile([P, XCH * D], BF16, name="x_sb%d" % c) for c in range(NT // XCH)]
+        b_sb = const.tile([P, 2 * F], BF16, name="b_sb")
+        w_sb = const.tile([P, 4, 2 * F], BF16, name="w_sb")
+        a_sb = const.tile([P, 4, R], BF16, name="a_sb")
+
+        def load_xa(c):
+            nc.sync.dma_start(out=xa_sb[c][:].rearrange("p (i r) -> p i r", r=R), in_=xa_v[:, 8 * c:8 * c + 8, :])
+
+        def load_x(c):
+            nc.sync.dma_start(out=x_sb[c][:].rearrange("p (i d) -> p i d", d=D), in_=x_v[:, XCH * c:XCH * c + XCH, :])
+
+        load_xa(0)
+        nc.sync.dma_start(out=b_sb[:], in_=B_gate_up)
+        for u in range(2):
+            nc.sync.dma_start(out=w_sb[:, 2 * u:2 * u + 2, :], in_=W_gate_up[256 * u:256 * u + 256, :].rearrange("(q e) c -> q e c", e=2))
+        load_x(0)
+        nc.sync.dma_start(out=a_sb[:], in_=A_down.rearrange("(t p) n -> p t n", p=P))
+        load_x(1)
+        load_xa(1)
+        load_x(2)
+        load_x(3)
+        load_xa(2)
+        load_x(4)
+        load_x(5)
+        load_xa(3)
+        load_x(6)
+        load_x(7)
+
+        xaT = {}
+        xt_ps = {}
+        xg = {}
+        xc = {}
+        xs = {}
+        l_ps = {}
+        l_sb = {}
+        m_ps = {}
+        g_sb = {}
+        u_sb = {}
+        s_sb = {}
+        h_sb = {}
+        ht_ps = {}
+        hg = {}
+        hc = {}
+        hs = {}
+        ha_ps = {}
+        wc = const.tile([P, 2 * F], U32, name="wc", align_bytes=64)
+        ws = const.tile([P, 2 * F], U8, name="ws", align_bytes=64)
+        ac = const.tile([P, R], U32, name="ac", align_bytes=64)
+        asc = const.tile([P, R], U8, name="asc", align_bytes=64)
+
+        def copy_on(eng, out, in_):
+            if eng == "S":
+                nc.scalar.copy(out=out, in_=in_)
+            else:
+                nc.vector.tensor_copy(out=out, in_=in_)
+
+        def XA(c):
+            t = ps.tile([P, 8, P], BF16, tag="ps", name="xat_ps")
+            for j in range(8):
+                nc.tensor.transpose(out=t[:, j, :], in_=xa_sb[c][:, R * j:R * j + R], identity=ident_b[:])
+            xaT[c] = const.tile([P, 8 * P], BF16, name="xaT%d" % c)
+            nc.scalar.copy(out=xaT[c][:], in_=t[:].rearrange("p j t -> p (j t)"))
+
+        def need_xa(t):
+            c = min(3, t // 8)
+            for cc in range(c + 1):
+                if cc not in xaT:
+                    XA(cc)
+
+        def w_prep():
+            wg = const.tile([P, 2 * F, 4], BF16, name="wg", align_bytes=64)
+            for hf in range(2):
+                nc.vector.tensor_copy(
+                    out=wg[:, F * hf:F * hf + F, :].rearrange("p (c i) t -> p c t i", i=4),
+                    in_=w_sb[:, :, F * hf:F * hf + F].rearrange("p t (c i) -> p c t i", i=4),
+                )
+            for hf in range(2):
+                nc.vector.quantize_mx(
+                    out=wc[:, F * hf:F * hf + F].bitcast(FP8X4),
+                    scales=ws[:, F * hf:F * hf + F],
+                    in_=wg[:, F * hf:F * hf + F, :].rearrange("p c t -> p (c t)"),
+                )
+            ag = const.tile([P, R, 4], BF16, name="ag", align_bytes=64)
+            nc.vector.tensor_copy(out=ag[:], in_=a_sb[:].rearrange("p t n -> p n t"))
+            nc.vector.quantize_mx(out=ac[:].bitcast(FP8X4), scales=asc[:], in_=ag[:].rearrange("p n t -> p (n t)"))
+
+        def XT(n):
+            if n < 0 or n >= NP:
+                return
+            t = ps.tile([P, 2, 2, P], F32, tag="ps", name="xt_ps")
+            xt_ps[n] = t
+            for j in range(2):
+                i = 2 * n + j
+                xw = x_sb[i // XCH][:].bitcast(F32)
+                base = (i % XCH) * (D // 2)
+                for u in range(2):
+                    nc.tensor.transpose(out=t[:, j, u, :], in_=xw[:, base + P * u:base + P * u + P], identity=ident_f[:])
+
+        def XTout(n, eng):
+            if n < 0 or n >= NP:
+                return
+            xg[n] = work.tile([P, 2 * P * 4], BF16, tag="xg", name="xg", align_bytes=64)
+            copy_on(
+                eng,
+                xg[n][:].bitcast(F32).rearrange("p (j t u) -> p j t u", j=2, u=2),
+                xt_ps[n][:].rearrange("p j u t -> p j t u"),
+            )
+
+        def qx(n):
+            if n < 0 or n >= NP:
+                return
+            xc[n] = const.tile([P, 2 * P], U32, name="xc%d" % n, align_bytes=64)
+            xs[n] = const.tile([P, 2 * P], U8, name="xs%d" % n, align_bytes=64)
+            nc.vector.quantize_mx(out=xc[n][:].bitcast(FP8X4), scales=xs[n][:], in_=xg[n][:])
+
+        def L(t, hf):
+            if t < 0 or t >= NT:
+                return
+            b = ps.tile([P, F], F32, tag="ps", name="l_ps")
+            l_ps[(t, hf)] = b
+            nc.tensor.matmul(out=b[:], lhsT=xaT[t // 8][:, P * (t % 8):P * (t % 8) + P], rhs=b_sb[:, F * hf:F * hf + F], start=True, stop=True)
+
+        def ad(t, hf):
+            if t < 0 or t >= NT:
+                return
+            l_sb[(t, hf)] = work.tile([P, F], F32, tag="ls", name="l_sb", bufs=LS_BUFS)
+            nc.scalar.copy(out=l_sb[(t, hf)][:], in_=l_ps[(t, hf)][:])
+
+        def M(t, hf):
+            if t < 0 or t >= NT:
+                return
+            b = ps.tile([P, F], F32, tag="ps", name="m_ps")
+            m_ps[(t, hf)] = b
+            n = t // 2
+            j = t % 2
+            nc.tensor.matmul_mx(
+                out=b[:],
+                lhsT=xc[n][:, P * j:P * j + P].bitcast(FP8X4),
+                lhsT_scale=xs[n][:, P * j:P * j + P],
+                rhs=wc[:, F * hf:F * hf + F].bitcast(FP8X4),
+                rhs_scale=ws[:, F * hf:F * hf + F],
+                start=True,
+                stop=True,
+            )
+
+        def be(t, hf):
+            if t < 0 or t >= NT:
+                return
+            o = work.tile([P, F], F32, tag="u" if hf else "g", name="gu_sb", bufs=4)
+            if hf:
+                u_sb[t] = o
+            else:
+                g_sb[t] = o
+            nc.vector.tensor_tensor(out=o[:], in0=m_ps[(t, hf)][:], in1=l_sb[(t, hf)][:], op=ADD)
+
+        def c_(t):
+            if t < 0 or t >= NT:
+                return
+            s_sb[t] = work.tile([P, F], F32, tag="s", name="s_sb", bufs=4)
+            nc.scalar.activation(out=s_sb[t][:], in_=g_sb[t][:], func=SILU)
+
+        def f_(t):
+            if t < 0 or t >= NT:
+                return
+            n = t // 2
+            j = t % 2
+            if j == 0:
+                h_sb[n] = work.tile([P, 2 * F], F32, tag="h", name="h_sb", bufs=4)
+            nc.gpsimd.tensor_tensor(out=h_sb[n][:, F * j:F * j + F], in0=s_sb[t][:], in1=u_sb[t][:], op=MULT)
+
+        def hst(n):
+            nc.sync.dma_start(out=h_v[:, 2 * n:2 * n + 2, :], in_=h_sb[n][:].rearrange("p (i f) -> p i f", f=F))
+
+        def HT(t):
+            if t < 0 or t >= NT:
+                return
+            b = ps.tile([P, 4, P], F32, tag="ps", name="ht_ps")
+            ht_ps[t] = b
+            n = t // 2
+            j = t % 2
+            for q in range(4):
+                nc.tensor.transpose(out=b[:, q, :], in_=h_sb[n][:, F * j + P * q:F * j + P * q + P], identity=ident_f[:])
+
+        def HTout(t, eng):
+            if t < 0 or t >= NT:
+                return
+            n = t // 2
+            j = t % 2
+            if j == 0:
+                hg[n] = work.tile([P, 2, P, 4], BF16, tag="hg", name="hg", align_bytes=64)
+            copy_on(eng, hg[n][:, j, :, :], ht_ps[t][:].rearrange("p q r -> p r q"))
+
+        def qh(n):
+            if n < 0 or n >= NP:
+                return
+            hc[n] = work.tile([P, 2 * P], U32, tag="hc", name="hc", align_bytes=64)
+            hs[n] = work.tile([P, 2 * P], U8, tag="hs", name="hs", align_bytes=64)
+            nc.vector.quantize_mx(out=hc[n][:].bitcast(FP8X4), scales=hs[n][:], in_=hg[n][:].rearrange("p j r q -> p (j r q)"))
+
+        def MX2(n):
+            if n < 0 or n >= NP:
+                return
+            b = ps.tile([P, 2, R], F32, tag="ps", name="ha_ps")
+            ha_ps[n] = b
+            for j in range(2):
+                nc.tensor.matmul_mx(
+                    out=b[:, j, :],
+                    lhsT=hc[n][:, P * j:P * j + P].bitcast(FP8X4),
+                    lhsT_scale=hs[n][:, P * j:P * j + P],
+                    rhs=ac[:].bitcast(FP8X4),
+                    rhs_scale=asc[:],
+                    start=True,
+                    stop=True,
+                )
+
+        def HAout(n, eng):
+            if n < 0 or n >= NP:
+                return
+            o = work.tile([P, 2, R], F32, tag="ha", name="ha_sb")
+            copy_on(eng, o[:], ha_ps[n][:])
+            nc.sync.dma_start(out=ha_v[:, 2 * n:2 * n + 2, :], in_=o[:])
+
+        need_xa(0)
+        for t in range(LL0):
+            L(t, 0)
+            L(t, 1)
+            ad(t, 0)
+            ad(t, 1)
+        for n in range(LX):
+            XT(n)
+            XTout(n, "S")
+        w_prep()
+        for n in range(LX):
+            qx(n)
+        for t in range(LL0, LL):
+            need_xa(t)
+            L(t, 0)
+            L(t, 1)
+            ad(t, 0)
+            ad(t, 1)
+
+        for n in range(NP + LH + 2):
+            A = 2 * n
+            B = A + 1
+            XT(n + LX)
+            if B + LL + 2 < NT + 2:
+                need_xa(min(NT - 1, B + LL + 2))
+            HT(2 * (n - LH))
+            HT(2 * (n - LH) + 1)
+            MX2(n - LH - 1)
+            XTout(n + LX, "S")
+            to_s = (n >= NP - TAIL_S) or (HT2S > 0 and n % HT2S == 0)
+            HTout(2 * (n - LH), "V")
+            HTout(2 * (n - LH) + 1, "S" if to_s else "V")
+            HAout(n - LH - 1, HA_ENG)
+            for t in (A, B):
+                M(t, 0)
+                M(t, 1)
+                L(t + LL, 0)
+                L(t + LL, 1)
+                be(t, 0)
+                ad(t + LL, 0)
+                be(t, 1)
+                ad(t + LL, 1)
+                c_(t)
+                f_(t)
+                if t == A:
+                    qh(n - LH)
+                else:
+                    qx(n + LX)
+            if B < NT:
+                hst(n)

@@ -20,14 +20,14 @@ NT = T // P
 NP = NT // 2
 FLOPS = 2 * T * D * 2 * F + 2 * T * R * 2 * F + 2 * T * F * R
 
-PIN = False
+PIN = True
 LX = 2
 LH = 2
 LL = 4
-LL0 = 2
+LL0 = 3
 XCH = 4
 LS_BUFS = 12
-TAIL_S = 2
+TAIL_S = 0
 HT2S = 0
 HA_ENG = "S"
 
@@ -138,6 +138,8 @@ def tile_loramlp_pa_t_kernel(tc, x, xa, W_gate_up, B_gate_up, A_down, out_0, out
                     scales=ws[:, F * hf:F * hf + F],
                     in_=wg[:, F * hf:F * hf + F, :].rearrange("p c t -> p (c t)"),
                 )
+
+        def a_prep():
             ag = const.tile([P, R, 4], BF16, name="ag", align_bytes=64)
             nc.vector.tensor_copy(out=ag[:], in_=a_sb[:].rearrange("p t n -> p n t"))
             nc.vector.quantize_mx(out=ac[:].bitcast(FP8X4), scales=asc[:], in_=ag[:].rearrange("p n t -> p (n t)"))
@@ -217,14 +219,17 @@ def tile_loramlp_pa_t_kernel(tc, x, xa, W_gate_up, B_gate_up, A_down, out_0, out
             s_sb[t] = work.tile([P, F], F32, tag="s", name="s_sb", bufs=4)
             nc.scalar.activation(out=s_sb[t][:], in_=g_sb[t][:], func=SILU)
 
-        def f_(t):
+        def f_(t, eng="G"):
             if t < 0 or t >= NT:
                 return
             n = t // 2
             j = t % 2
             if j == 0:
                 h_sb[n] = work.tile([P, 2 * F], F32, tag="h", name="h_sb", bufs=4)
-            nc.gpsimd.tensor_tensor(out=h_sb[n][:, F * j:F * j + F], in0=s_sb[t][:], in1=u_sb[t][:], op=MULT)
+            if eng == "G":
+                nc.gpsimd.tensor_tensor(out=h_sb[n][:, F * j:F * j + F], in0=s_sb[t][:], in1=u_sb[t][:], op=MULT)
+            else:
+                nc.vector.tensor_tensor(out=h_sb[n][:, F * j:F * j + F], in0=s_sb[t][:], in1=u_sb[t][:], op=MULT)
 
         def hst(n):
             nc.sync.dma_start(out=h_v[:, 2 * n:2 * n + 2, :], in_=h_sb[n][:].rearrange("p (i f) -> p i f", f=F))
@@ -274,7 +279,7 @@ def tile_loramlp_pa_t_kernel(tc, x, xa, W_gate_up, B_gate_up, A_down, out_0, out
         def HAout(n, eng):
             if n < 0 or n >= NP:
                 return
-            o = work.tile([P, 2, R], F32, tag="ha", name="ha_sb")
+            o = work.tile([P, 2, R], F32, tag="ha", name="ha_sb", bufs=6)
             copy_on(eng, o[:], ha_ps[n][:])
             nc.sync.dma_start(out=ha_v[:, 2 * n:2 * n + 2, :], in_=o[:])
 
@@ -290,6 +295,7 @@ def tile_loramlp_pa_t_kernel(tc, x, xa, W_gate_up, B_gate_up, A_down, out_0, out
         w_prep()
         for n in range(LX):
             qx(n)
+        a_prep()
         for t in range(LL0, LL):
             need_xa(t)
             L(t, 0)
@@ -297,7 +303,7 @@ def tile_loramlp_pa_t_kernel(tc, x, xa, W_gate_up, B_gate_up, A_down, out_0, out
             ad(t, 0)
             ad(t, 1)
 
-        for n in range(NP + LH + 2):
+        for n in range(NP - 2):
             A = 2 * n
             B = A + 1
             XT(n + LX)
@@ -307,10 +313,9 @@ def tile_loramlp_pa_t_kernel(tc, x, xa, W_gate_up, B_gate_up, A_down, out_0, out
             HT(2 * (n - LH) + 1)
             MX2(n - LH - 1)
             XTout(n + LX, "S")
-            to_s = (n >= NP - TAIL_S) or (HT2S > 0 and n % HT2S == 0)
             HTout(2 * (n - LH), "V")
-            HTout(2 * (n - LH) + 1, "S" if to_s else "V")
-            HAout(n - LH - 1, HA_ENG)
+            HTout(2 * (n - LH) + 1, "V")
+            HAout(n - LH - 1, "V" if n % 2 else "S")
             for t in (A, B):
                 M(t, 0)
                 M(t, 1)
@@ -326,5 +331,61 @@ def tile_loramlp_pa_t_kernel(tc, x, xa, W_gate_up, B_gate_up, A_down, out_0, out
                     qh(n - LH)
                 else:
                     qx(n + LX)
-            if B < NT:
-                hst(n)
+            hst(n)
+
+        def M2(t):
+            M(t, 0)
+            M(t, 1)
+
+        def BE(t):
+            be(t, 0)
+            be(t, 1)
+
+        M2(28)
+        M2(29)
+        HT(24)
+        HT(25)
+        MX2(11)
+        BE(28)
+        HTout(24, "S")
+        c_(28)
+        f_(28)
+        HTout(25, "S")
+        M2(30)
+        BE(29)
+        c_(29)
+        f_(29)
+        hst(14)
+        HAout(11, "S")
+        M2(31)
+        HT(26)
+        HT(27)
+        BE(30)
+        qh(12)
+        c_(30)
+        f_(30)
+        HTout(26, "S")
+        MX2(12)
+        BE(31)
+        c_(31)
+        HTout(27, "S")
+        f_(31, "V")
+        hst(15)
+        HAout(12, "S")
+        HT(28)
+        HT(29)
+        HTout(28, "S")
+        qh(13)
+        HTout(29, "V")
+        HT(30)
+        HT(31)
+        MX2(13)
+        HTout(30, "S")
+        HTout(31, "V")
+        HAout(13, "S")
+        qh(14)
+        qh(15)
+        MX2(14)
+        MX2(15)
+        HAout(14, "S")
+        HAout(15, "V")

@@ -250,7 +250,7 @@ def tile_loramlp_pa_t_kernel(tc, x, xa, W_gate_up, B_gate_up, A_down, out_0, out
             n = t // 2
             j = t % 2
             if j == 0:
-                hg[n] = work.tile([P, 2, P, 4], BF16, tag="hg", name="hg", align_bytes=64)
+                hg[n] = work.tile([P, 2, P, 4], BF16, tag="hg", name="hg", align_bytes=64, bufs=6)
             copy_on(eng, hg[n][:, j, :, :], ht_ps[t][:].rearrange("p q r -> p r q"))
 
         def qh(n):
@@ -306,31 +306,38 @@ def tile_loramlp_pa_t_kernel(tc, x, xa, W_gate_up, B_gate_up, A_down, out_0, out
         for n in range(NP - 2):
             A = 2 * n
             B = A + 1
+            M(A, 0)
+            M(A, 1)
+            L(A + LL, 0)
+            L(A + LL, 1)
+            M(B, 0)
+            be(A, 0)
+            ad(A + LL, 0)
+            be(A, 1)
+            ad(A + LL, 1)
+            c_(A)
+            f_(A)
             XT(n + LX)
             if B + LL + 2 < NT + 2:
                 need_xa(min(NT - 1, B + LL + 2))
             HT(2 * (n - LH))
             HT(2 * (n - LH) + 1)
-            MX2(n - LH - 1)
-            XTout(n + LX, "S")
+            MX2(n - LH - 2)
+            be(B, 0)
+            XTout(n + LX, "V" if n < LH else "S")
             HTout(2 * (n - LH), "V")
             HTout(2 * (n - LH) + 1, "V")
-            HAout(n - LH - 1, "V" if n % 2 else "S")
-            for t in (A, B):
-                M(t, 0)
-                M(t, 1)
-                L(t + LL, 0)
-                L(t + LL, 1)
-                be(t, 0)
-                ad(t + LL, 0)
-                be(t, 1)
-                ad(t + LL, 1)
-                c_(t)
-                f_(t)
-                if t == A:
-                    qh(n - LH)
-                else:
-                    qx(n + LX)
+            M(B, 1)
+            L(B + LL, 0)
+            L(B + LL, 1)
+            c_(B)
+            HAout(n - LH - 2, "V" if n % 2 else "S")
+            qh(n - LH - 1)
+            qx(n + LX)
+            ad(B + LL, 0)
+            be(B, 1)
+            ad(B + LL, 1)
+            f_(B)
             hst(n)
 
         def M2(t):
@@ -345,47 +352,50 @@ def tile_loramlp_pa_t_kernel(tc, x, xa, W_gate_up, B_gate_up, A_down, out_0, out
         M2(29)
         HT(24)
         HT(25)
-        MX2(11)
+        MX2(10)
         BE(28)
         HTout(24, "S")
         c_(28)
         f_(28)
         HTout(25, "S")
+        HAout(10, "S")
         M2(30)
         BE(29)
         c_(29)
         f_(29)
         hst(14)
-        HAout(11, "S")
         M2(31)
         HT(26)
         HT(27)
         BE(30)
-        qh(12)
         c_(30)
         f_(30)
         HTout(26, "S")
-        MX2(12)
         BE(31)
         c_(31)
         HTout(27, "S")
         f_(31, "V")
         hst(15)
-        HAout(12, "S")
         HT(28)
         HT(29)
         HTout(28, "S")
+        HTout(29, "S")
+        qh(11)
+        qh(12)
+        MX2(11)
+        MX2(12)
         qh(13)
-        HTout(29, "V")
+        qh(14)
         HT(30)
         HT(31)
-        MX2(13)
         HTout(30, "S")
         HTout(31, "V")
-        HAout(13, "S")
-        qh(14)
-        qh(15)
+        MX2(13)
         MX2(14)
-        MX2(15)
+        HAout(11, "S")
+        HAout(12, "S")
+        qh(15)
+        HAout(13, "S")
         HAout(14, "S")
+        MX2(15)
         HAout(15, "V")

@@ -125,19 +125,20 @@ def tile_loramlp_pa_t_kernel(tc, x, xa, W_gate_up, B_gate_up, A_down, out_0, out
                 if cc not in xaT:
                     XA(cc)
 
-        def w_prep():
-            wg = const.tile([P, 2 * F, 4], BF16, name="wg", align_bytes=64)
-            for hf in range(2):
-                nc.vector.tensor_copy(
-                    out=wg[:, F * hf:F * hf + F, :].rearrange("p (c i) t -> p c t i", i=4),
-                    in_=w_sb[:, :, F * hf:F * hf + F].rearrange("p t (c i) -> p c t i", i=4),
-                )
-            for hf in range(2):
-                nc.vector.quantize_mx(
-                    out=wc[:, F * hf:F * hf + F].bitcast(FP8X4),
-                    scales=ws[:, F * hf:F * hf + F],
-                    in_=wg[:, F * hf:F * hf + F, :].rearrange("p c t -> p (c t)"),
-                )
+        wg = const.tile([P, 2 * F, 4], BF16, name="wg", align_bytes=64)
+
+        def w_rg(hf):
+            nc.vector.tensor_copy(
+                out=wg[:, F * hf:F * hf + F, :].rearrange("p (c i) t -> p c t i", i=4),
+                in_=w_sb[:, :, F * hf:F * hf + F].rearrange("p t (c i) -> p c t i", i=4),
+            )
+
+        def w_q(hf):
+            nc.vector.quantize_mx(
+                out=wc[:, F * hf:F * hf + F].bitcast(FP8X4),
+                scales=ws[:, F * hf:F * hf + F],
+                in_=wg[:, F * hf:F * hf + F, :].rearrange("p c t -> p (c t)"),
+            )
 
         def a_prep():
             ag = const.tile([P, R, 4], BF16, name="ag", align_bytes=64)
@@ -206,18 +207,25 @@ def tile_loramlp_pa_t_kernel(tc, x, xa, W_gate_up, B_gate_up, A_down, out_0, out
         def be(t, hf):
             if t < 0 or t >= NT:
                 return
-            o = work.tile([P, F], F32, tag="u" if hf else "g", name="gu_sb", bufs=4)
+            n = t // 2
+            j = t % 2
             if hf:
-                u_sb[t] = o
+                if j == 0:
+                    u_sb[n] = work.tile([P, 2 * F], F32, tag="u", name="u_sb", bufs=3)
+                o = u_sb[n][:, F * j:F * j + F]
             else:
-                g_sb[t] = o
-            nc.vector.tensor_tensor(out=o[:], in0=m_ps[(t, hf)][:], in1=l_sb[(t, hf)][:], op=ADD)
+                g_sb[t] = work.tile([P, F], F32, tag="g", name="g_sb", bufs=4)
+                o = g_sb[t][:]
+            nc.vector.tensor_tensor(out=o, in0=m_ps[(t, hf)][:], in1=l_sb[(t, hf)][:], op=ADD)
 
         def c_(t):
             if t < 0 or t >= NT:
                 return
-            s_sb[t] = work.tile([P, F], F32, tag="s", name="s_sb", bufs=4)
-            nc.scalar.activation(out=s_sb[t][:], in_=g_sb[t][:], func=SILU)
+            n = t // 2
+            j = t % 2
+            if j == 0:
+                s_sb[n] = work.tile([P, 2 * F], F32, tag="s", name="s_sb", bufs=3)
+            nc.scalar.activation(out=s_sb[n][:, F * j:F * j + F], in_=g_sb[t][:], func=SILU)
 
         def f_(t, eng="G"):
             if t < 0 or t >= NT:
@@ -226,10 +234,15 @@ def tile_loramlp_pa_t_kernel(tc, x, xa, W_gate_up, B_gate_up, A_down, out_0, out
             j = t % 2
             if j == 0:
                 h_sb[n] = work.tile([P, 2 * F], F32, tag="h", name="h_sb", bufs=4)
+            cols = slice(F * j, F * j + F)
             if eng == "G":
-                nc.gpsimd.tensor_tensor(out=h_sb[n][:, F * j:F * j + F], in0=s_sb[t][:], in1=u_sb[t][:], op=MULT)
+                nc.gpsimd.tensor_tensor(out=h_sb[n][:, cols], in0=s_sb[n][:, cols], in1=u_sb[n][:, cols], op=MULT)
             else:
-                nc.vector.tensor_tensor(out=h_sb[n][:, F * j:F * j + F], in0=s_sb[t][:], in1=u_sb[t][:], op=MULT)
+                nc.vector.tensor_tensor(out=h_sb[n][:, cols], in0=s_sb[n][:, cols], in1=u_sb[n][:, cols], op=MULT)
+
+        def f2(n):
+            h_sb[n] = work.tile([P, 2 * F], F32, tag="h", name="h_sb", bufs=4)
+            nc.gpsimd.tensor_tensor(out=h_sb[n][:], in0=s_sb[n][:], in1=u_sb[n][:], op=MULT)
 
         def hst(n):
             nc.sync.dma_start(out=h_v[:, 2 * n:2 * n + 2, :], in_=h_sb[n][:].rearrange("p (i f) -> p i f", f=F))
@@ -284,24 +297,28 @@ def tile_loramlp_pa_t_kernel(tc, x, xa, W_gate_up, B_gate_up, A_down, out_0, out
             nc.sync.dma_start(out=ha_v[:, 2 * n:2 * n + 2, :], in_=o[:])
 
         need_xa(0)
-        for t in range(LL0):
+        for t in range(2):
             L(t, 0)
             L(t, 1)
             ad(t, 0)
             ad(t, 1)
-        for n in range(LX):
-            XT(n)
-            XTout(n, "S")
-        w_prep()
-        for n in range(LX):
-            qx(n)
-        a_prep()
-        for t in range(LL0, LL):
-            need_xa(t)
-            L(t, 0)
-            L(t, 1)
-            ad(t, 0)
-            ad(t, 1)
+        L(2, 0)
+        L(2, 1)
+        ad(2, 0)
+        XT(0)
+        XTout(0, "S")
+        ad(2, 1)
+        XT(1)
+        XTout(1, "S")
+        w_rg(0)
+        w_rg(1)
+        w_q(0)
+        qx(0)
+        w_q(1)
+        L(3, 0)
+        L(3, 1)
+        ad(3, 0)
+        ad(3, 1)
 
         for n in range(NP - 2):
             A = 2 * n
@@ -316,7 +333,6 @@ def tile_loramlp_pa_t_kernel(tc, x, xa, W_gate_up, B_gate_up, A_down, out_0, out
             be(A, 1)
             ad(A + LL, 1)
             c_(A)
-            f_(A)
             XT(n + LX)
             if B + LL + 2 < NT + 2:
                 need_xa(min(NT - 1, B + LL + 2))
@@ -332,12 +348,16 @@ def tile_loramlp_pa_t_kernel(tc, x, xa, W_gate_up, B_gate_up, A_down, out_0, out
             L(B + LL, 1)
             c_(B)
             HAout(n - LH - 2, "V" if n % 2 else "S")
+            if n == 0:
+                qx(1)
+            if n == 1:
+                a_prep()
             qh(n - LH - 1)
             qx(n + LX)
             ad(B + LL, 0)
             be(B, 1)
             ad(B + LL, 1)
-            f_(B)
+            f2(n)
             hst(n)
 
         def M2(t):

@@ -72,10 +72,10 @@ def tile_loramlp_pa_t_kernel(tc, x, xa, W_gate_up, B_gate_up, A_down, out_0, out
         for u in range(2):
             nc.sync.dma_start(out=w_sb[:, 2 * u:2 * u + 2, :], in_=W_gate_up[256 * u:256 * u + 256, :].rearrange("(q e) c -> q e c", e=2))
         load_x(0)
-        nc.sync.dma_start(out=a_sb[:], in_=A_down.rearrange("(t p) n -> p t n", p=P))
         load_x(1)
         load_xa(1)
         load_x(2)
+        nc.sync.dma_start(out=a_sb[:], in_=A_down.rearrange("(t p) n -> p t n", p=P))
         load_x(3)
         load_xa(2)
         load_x(4)
@@ -389,33 +389,33 @@ def tile_loramlp_pa_t_kernel(tc, x, xa, W_gate_up, B_gate_up, A_down, out_0, out
         HT(27)
         BE(30)
         c_(30)
-        f_(30)
         HTout(26, "S")
         BE(31)
         c_(31)
         HTout(27, "S")
+        f_(30, "V")
         f_(31, "V")
         hst(15)
         HT(28)
         HT(29)
         HTout(28, "S")
         HTout(29, "S")
+        HT(30)
+        HT(31)
         qh(11)
         qh(12)
+        HTout(30, "S")
+        HTout(31, "V")
         MX2(11)
         MX2(12)
         qh(13)
         qh(14)
-        HT(30)
-        HT(31)
-        HTout(30, "S")
-        HTout(31, "V")
-        MX2(13)
-        MX2(14)
+        qh(15)
         HAout(11, "S")
         HAout(12, "S")
-        qh(15)
-        HAout(13, "S")
-        HAout(14, "S")
+        MX2(13)
+        MX2(14)
         MX2(15)
-        HAout(15, "V")
+        HAout(13, "S")
+        HAout(14, "V")
+        HAout(15, "S")

@@ -56,33 +56,47 @@ def tile_loramlp_pa_t_kernel(tc, x, xa, W_gate_up, B_gate_up, A_down, out_0, out
         make_identity(nc, ident_f[:])
 
         xa_sb = [const.tile([P, 8 * R], BF16, name="xa_sb%d" % c) for c in range(4)]
-        x_sb = [const.tile([P, XCH * D], BF16, name="x_sb%d" % c) for c in range(NT // XCH)]
+        x_chunks = [(0, 2), (2, 2)] + [(i0, 4) for i0 in range(4, NT, 4)]
+        x_sb = [const.tile([P, cnt * D], BF16, name="x_sb%d" % c) for c, (i0, cnt) in enumerate(x_chunks)]
+        x_of = {}
+        for c, (i0, cnt) in enumerate(x_chunks):
+            for k in range(cnt):
+                x_of[i0 + k] = (c, k)
         b_sb = const.tile([P, 2 * F], BF16, name="b_sb")
-        w_sb = const.tile([P, 4, 2 * F], BF16, name="w_sb")
+        w_sb = [const.tile([P, 4, F], BF16, name="w_sb%d" % hf) for hf in range(2)]
         a_sb = const.tile([P, 4, R], BF16, name="a_sb")
 
         def load_xa(c):
             nc.sync.dma_start(out=xa_sb[c][:].rearrange("p (i r) -> p i r", r=R), in_=xa_v[:, 8 * c:8 * c + 8, :])
 
         def load_x(c):
-            nc.sync.dma_start(out=x_sb[c][:].rearrange("p (i d) -> p i d", d=D), in_=x_v[:, XCH * c:XCH * c + XCH, :])
+            i0, cnt = x_chunks[c]
+            nc.sync.dma_start(out=x_sb[c][:].rearrange("p (i d) -> p i d", d=D), in_=x_v[:, i0:i0 + cnt, :])
+
+        def load_w(hf):
+            for u in range(2):
+                nc.sync.dma_start(
+                    out=w_sb[hf][:, 2 * u:2 * u + 2, :],
+                    in_=W_gate_up[256 * u:256 * u + 256, F * hf:F * hf + F].rearrange("(q e) c -> q e c", e=2),
+                )
 
         load_xa(0)
         nc.sync.dma_start(out=b_sb[:], in_=B_gate_up)
-        for u in range(2):
-            nc.sync.dma_start(out=w_sb[:, 2 * u:2 * u + 2, :], in_=W_gate_up[256 * u:256 * u + 256, :].rearrange("(q e) c -> q e c", e=2))
+        load_w(0)
         load_x(0)
+        load_w(1)
         load_x(1)
-        load_xa(1)
         load_x(2)
-        nc.sync.dma_start(out=a_sb[:], in_=A_down.rearrange("(t p) n -> p t n", p=P))
+        load_xa(1)
         load_x(3)
-        load_xa(2)
+        nc.sync.dma_start(out=a_sb[:], in_=A_down.rearrange("(t p) n -> p t n", p=P))
         load_x(4)
+        load_xa(2)
         load_x(5)
-        load_xa(3)
         load_x(6)
+        load_xa(3)
         load_x(7)
+        load_x(8)
 
         xaT = {}
         xt_ps = {}
@@ -130,7 +144,7 @@ def tile_loramlp_pa_t_kernel(tc, x, xa, W_gate_up, B_gate_up, A_down, out_0, out
         def w_rg(hf):
             nc.vector.tensor_copy(
                 out=wg[:, F * hf:F * hf + F, :].rearrange("p (c i) t -> p c t i", i=4),
-                in_=w_sb[:, :, F * hf:F * hf + F].rearrange("p t (c i) -> p c t i", i=4),
+                in_=w_sb[hf][:].rearrange("p t (c i) -> p c t i", i=4),
             )
 
         def w_q(hf):
@@ -152,8 +166,8 @@ def tile_loramlp_pa_t_kernel(tc, x, xa, W_gate_up, B_gate_up, A_down, out_0, out
             xt_ps[n] = t
             for j in range(2):
                 i = 2 * n + j
-                xw = x_sb[i // XCH][:].bitcast(F32)
-                base = (i % XCH) * (D // 2)
+                xw = x_sb[x_of[i][0]][:].bitcast(F32)
+                base = x_of[i][1] * (D // 2)
                 for u in range(2):
                     nc.tensor.transpose(out=t[:, j, u, :], in_=xw[:, base + P * u:base + P * u + P], identity=ident_f[:])
 
@@ -181,11 +195,11 @@ def tile_loramlp_pa_t_kernel(tc, x, xa, W_gate_up, B_gate_up, A_down, out_0, out
             l_ps[(t, hf)] = b
             nc.tensor.matmul(out=b[:], lhsT=xaT[t // 8][:, P * (t % 8):P * (t % 8) + P], rhs=b_sb[:, F * hf:F * hf + F], start=True, stop=True)
 
-        def ad(t, hf):
+        def ad(t, hf, eng="S"):
             if t < 0 or t >= NT:
                 return
             l_sb[(t, hf)] = work.tile([P, F], F32, tag="ls", name="l_sb", bufs=LS_BUFS)
-            nc.scalar.copy(out=l_sb[(t, hf)][:], in_=l_ps[(t, hf)][:])
+            copy_on(eng, l_sb[(t, hf)][:], l_ps[(t, hf)][:])
 
         def M(t, hf):
             if t < 0 or t >= NT:
@@ -297,23 +311,26 @@ def tile_loramlp_pa_t_kernel(tc, x, xa, W_gate_up, B_gate_up, A_down, out_0, out
             nc.sync.dma_start(out=ha_v[:, 2 * n:2 * n + 2, :], in_=o[:])
 
         need_xa(0)
-        for t in range(2):
-            L(t, 0)
-            L(t, 1)
-            ad(t, 0)
-            ad(t, 1)
+        L(0, 0)
+        L(0, 1)
+        ad(0, 0)
+        ad(0, 1)
+        w_rg(0)
+        L(1, 0)
+        L(1, 1)
+        ad(1, 0)
+        XT(0)
+        XTout(0, "S")
+        ad(1, 1)
+        w_q(0)
+        w_rg(1)
+        qx(0)
         L(2, 0)
         L(2, 1)
         ad(2, 0)
-        XT(0)
-        XTout(0, "S")
         ad(2, 1)
         XT(1)
         XTout(1, "S")
-        w_rg(0)
-        w_rg(1)
-        w_q(0)
-        qx(0)
         w_q(1)
         L(3, 0)
         L(3, 1)
@@ -331,7 +348,7 @@ def tile_loramlp_pa_t_kernel(tc, x, xa, W_gate_up, B_gate_up, A_down, out_0, out
             be(A, 0)
             ad(A + LL, 0)
             be(A, 1)
-            ad(A + LL, 1)
+            ad(A + LL, 1, "V" if n < LH else "S")
             c_(A)
             XT(n + LX)
             if B + LL + 2 < NT + 2:

@@ -22,7 +22,7 @@ FLOPS = 2 * T * D * 2 * F + 2 * T * R * 2 * F + 2 * T * F * R
 
 PIN = True
 LX = 2
-LH = 2
+LH = 3
 LL = 4
 LL0 = 3
 XCH = 4
@@ -55,19 +55,28 @@ def tile_loramlp_pa_t_kernel(tc, x, xa, W_gate_up, B_gate_up, A_down, out_0, out
         ident_f = const.tile([P, P], F32, name="ident_f")
         make_identity(nc, ident_f[:])
 
-        xa_sb = [const.tile([P, 8 * R], BF16, name="xa_sb%d" % c) for c in range(4)]
+        xa_chunks = [(0, 4), (4, 4), (8, 8), (16, 8), (24, 8)]
+        xa_sb = [const.tile([P, cnt * R], BF16, name="xa_sb%d" % c) for c, (i0, cnt) in enumerate(xa_chunks)]
+        xa_of = {}
+        for c, (i0, cnt) in enumerate(xa_chunks):
+            for k in range(cnt):
+                xa_of[i0 + k] = (c, k)
         x_chunks = [(0, 2), (2, 2)] + [(i0, 4) for i0 in range(4, NT, 4)]
         x_sb = [const.tile([P, cnt * D], BF16, name="x_sb%d" % c) for c, (i0, cnt) in enumerate(x_chunks)]
         x_of = {}
         for c, (i0, cnt) in enumerate(x_chunks):
             for k in range(cnt):
                 x_of[i0 + k] = (c, k)
-        b_sb = const.tile([P, 2 * F], BF16, name="b_sb")
+        b_sb = [const.tile([P, F], BF16, name="b_sb%d" % hf) for hf in range(2)]
         w_sb = [const.tile([P, 4, F], BF16, name="w_sb%d" % hf) for hf in range(2)]
         a_sb = const.tile([P, 4, R], BF16, name="a_sb")
 
         def load_xa(c):
-            nc.sync.dma_start(out=xa_sb[c][:].rearrange("p (i r) -> p i r", r=R), in_=xa_v[:, 8 * c:8 * c + 8, :])
+            i0, cnt = xa_chunks[c]
+            nc.sync.dma_start(out=xa_sb[c][:].rearrange("p (i r) -> p i r", r=R), in_=xa_v[:, i0:i0 + cnt, :])
+
+        def load_b(hf):
+            nc.sync.dma_start(out=b_sb[hf][:], in_=B_gate_up[:, F * hf:F * hf + F])
 
         def load_x(c):
             i0, cnt = x_chunks[c]
@@ -81,20 +90,22 @@ def tile_loramlp_pa_t_kernel(tc, x, xa, W_gate_up, B_gate_up, A_down, out_0, out
                 )
 
         load_xa(0)
-        nc.sync.dma_start(out=b_sb[:], in_=B_gate_up)
+        load_b(0)
         load_w(0)
         load_x(0)
+        load_b(1)
         load_w(1)
         load_x(1)
-        load_x(2)
         load_xa(1)
+        load_x(2)
+        load_xa(2)
         load_x(3)
         nc.sync.dma_start(out=a_sb[:], in_=A_down.rearrange("(t p) n -> p t n", p=P))
         load_x(4)
-        load_xa(2)
+        load_xa(3)
         load_x(5)
         load_x(6)
-        load_xa(3)
+        load_xa(4)
         load_x(7)
         load_x(8)
 
@@ -110,6 +121,7 @@ def tile_loramlp_pa_t_kernel(tc, x, xa, W_gate_up, B_gate_up, A_down, out_0, out
         u_sb = {}
         s_sb = {}
         h_sb = {}
+        h16 = {}
         ht_ps = {}
         hg = {}
         hc = {}
@@ -127,15 +139,15 @@ def tile_loramlp_pa_t_kernel(tc, x, xa, W_gate_up, B_gate_up, A_down, out_0, out
                 nc.vector.tensor_copy(out=out, in_=in_)
 
         def XA(c):
-            t = ps.tile([P, 8, P], BF16, tag="ps", name="xat_ps")
-            for j in range(8):
+            cnt = xa_chunks[c][1]
+            t = ps.tile([P, cnt, P], BF16, tag="ps", name="xat_ps")
+            for j in range(cnt):
                 nc.tensor.transpose(out=t[:, j, :], in_=xa_sb[c][:, R * j:R * j + R], identity=ident_b[:])
-            xaT[c] = const.tile([P, 8 * P], BF16, name="xaT%d" % c)
+            xaT[c] = const.tile([P, cnt * P], BF16, name="xaT%d" % c)
             nc.scalar.copy(out=xaT[c][:], in_=t[:].rearrange("p j t -> p (j t)"))
 
         def need_xa(t):
-            c = min(3, t // 8)
-            for cc in range(c + 1):
+            for cc in range(xa_of[t][0] + 1):
                 if cc not in xaT:
                     XA(cc)
 
@@ -193,7 +205,8 @@ def tile_loramlp_pa_t_kernel(tc, x, xa, W_gate_up, B_gate_up, A_down, out_0, out
                 return
             b = ps.tile([P, F], F32, tag="ps", name="l_ps")
             l_ps[(t, hf)] = b
-            nc.tensor.matmul(out=b[:], lhsT=xaT[t // 8][:, P * (t % 8):P * (t % 8) + P], rhs=b_sb[:, F * hf:F * hf + F], start=True, stop=True)
+            c, k = xa_of[t]
+            nc.tensor.matmul(out=b[:], lhsT=xaT[c][:, P * k:P * k + P], rhs=b_sb[hf][:], start=True, stop=True)
 
         def ad(t, hf, eng="S"):
             if t < 0 or t >= NT:
@@ -247,7 +260,7 @@ def tile_loramlp_pa_t_kernel(tc, x, xa, W_gate_up, B_gate_up, A_down, out_0, out
             n = t // 2
             j = t % 2
             if j == 0:
-                h_sb[n] = work.tile([P, 2 * F], F32, tag="h", name="h_sb", bufs=4)
+                h_sb[n] = work.tile([P, 2 * F], F32, tag="h", name="h_sb", bufs=6)
             cols = slice(F * j, F * j + F)
             if eng == "G":
                 nc.gpsimd.tensor_tensor(out=h_sb[n][:, cols], in0=s_sb[n][:, cols], in1=u_sb[n][:, cols], op=MULT)
@@ -255,8 +268,19 @@ def tile_loramlp_pa_t_kernel(tc, x, xa, W_gate_up, B_gate_up, A_down, out_0, out
                 nc.vector.tensor_tensor(out=h_sb[n][:, cols], in0=s_sb[n][:, cols], in1=u_sb[n][:, cols], op=MULT)
 
         def f2(n):
-            h_sb[n] = work.tile([P, 2 * F], F32, tag="h", name="h_sb", bufs=4)
+            h_sb[n] = work.tile([P, 2 * F], F32, tag="h", name="h_sb", bufs=6)
             nc.gpsimd.tensor_tensor(out=h_sb[n][:], in0=s_sb[n][:], in1=u_sb[n][:], op=MULT)
+
+        def rA(n):
+            h16[n] = work.tile([P, 2, P, 2], BF16, tag="h16", name="h16", bufs=4)
+            nc.gpsimd.tensor_scalar(
+                out=h16[n][:],
+                in0=h_sb[n][:, 0:F].rearrange("p (u e c) -> p u c e", u=2, e=2),
+                scalar1=1.0,
+                scalar2=0.0,
+                op0=MULT,
+                op1=ADD,
+            )
 
         def hst(n):
             nc.sync.dma_start(out=h_v[:, 2 * n:2 * n + 2, :], in_=h_sb[n][:].rearrange("p (i f) -> p i f", f=F))
@@ -264,12 +288,18 @@ def tile_loramlp_pa_t_kernel(tc, x, xa, W_gate_up, B_gate_up, A_down, out_0, out
         def HT(t):
             if t < 0 or t >= NT:
                 return
-            b = ps.tile([P, 4, P], F32, tag="ps", name="ht_ps")
-            ht_ps[t] = b
             n = t // 2
             j = t % 2
-            for q in range(4):
-                nc.tensor.transpose(out=b[:, q, :], in_=h_sb[n][:, F * j + P * q:F * j + P * q + P], identity=ident_f[:])
+            if n in h16 and j == 0:
+                b = ps.tile([P, 2, P], F32, tag="ps", name="ht_ps")
+                hw = h16[n][:].rearrange("p u c e -> p (u c e)").bitcast(F32)
+                for u in range(2):
+                    nc.tensor.transpose(out=b[:, u, :], in_=hw[:, P * u:P * u + P], identity=ident_f[:])
+            else:
+                b = ps.tile([P, 4, P], F32, tag="ps", name="ht_ps")
+                for q in range(4):
+                    nc.tensor.transpose(out=b[:, q, :], in_=h_sb[n][:, F * j + P * q:F * j + P * q + P], identity=ident_f[:])
+            ht_ps[t] = b
 
         def HTout(t, eng):
             if t < 0 or t >= NT:
@@ -278,7 +308,14 @@ def tile_loramlp_pa_t_kernel(tc, x, xa, W_gate_up, B_gate_up, A_down, out_0, out
             j = t % 2
             if j == 0:
                 hg[n] = work.tile([P, 2, P, 4], BF16, tag="hg", name="hg", align_bytes=64, bufs=6)
-            copy_on(eng, hg[n][:, j, :, :], ht_ps[t][:].rearrange("p q r -> p r q"))
+            if n in h16 and j == 0:
+                copy_on(
+                    eng,
+                    hg[n][:, 0, :, :].rearrange("p r k -> p (r k)").bitcast(F32).rearrange("p (r u) -> p r u", u=2),
+                    ht_ps[t][:].rearrange("p u r -> p r u"),
+                )
+            else:
+                copy_on(eng, hg[n][:, j, :, :], ht_ps[t][:].rearrange("p q r -> p r q"))
 
         def qh(n):
             if n < 0 or n >= NP:
@@ -312,28 +349,29 @@ def tile_loramlp_pa_t_kernel(tc, x, xa, W_gate_up, B_gate_up, A_down, out_0, out
 
         need_xa(0)
         L(0, 0)
-        L(0, 1)
-        ad(0, 0)
-        ad(0, 1)
-        w_rg(0)
         L(1, 0)
-        L(1, 1)
+        ad(0, 0)
         ad(1, 0)
+        w_rg(0)
+        L(2, 0)
+        ad(2, 0)
         XT(0)
         XTout(0, "S")
-        ad(1, 1)
+        L(0, 1)
+        L(1, 1)
         w_q(0)
         w_rg(1)
         qx(0)
-        L(2, 0)
+        ad(0, 1)
+        ad(1, 1)
         L(2, 1)
-        ad(2, 0)
         ad(2, 1)
         XT(1)
         XTout(1, "S")
         w_q(1)
         L(3, 0)
         L(3, 1)
+        need_xa(4)
         ad(3, 0)
         ad(3, 1)
 
@@ -348,34 +386,37 @@ def tile_loramlp_pa_t_kernel(tc, x, xa, W_gate_up, B_gate_up, A_down, out_0, out
             be(A, 0)
             ad(A + LL, 0)
             be(A, 1)
-            ad(A + LL, 1, "V" if n < LH else "S")
+            ad(A + LL, 1, "V" if n < 2 else "S")
             c_(A)
             XT(n + LX)
             if B + LL + 2 < NT + 2:
                 need_xa(min(NT - 1, B + LL + 2))
             HT(2 * (n - LH))
             HT(2 * (n - LH) + 1)
-            MX2(n - LH - 2)
+            MX2(n - LH - 1)
             be(B, 0)
-            XTout(n + LX, "V" if n < LH else "S")
+            XTout(n + LX, "V" if n < 2 else "S")
             HTout(2 * (n - LH), "V")
             HTout(2 * (n - LH) + 1, "V")
             M(B, 1)
             L(B + LL, 0)
             L(B + LL, 1)
             c_(B)
-            HAout(n - LH - 2, "V" if n % 2 else "S")
+            HAout(n - LH - 1, "V")
             if n == 0:
                 qx(1)
             if n == 1:
                 a_prep()
-            qh(n - LH - 1)
-            qx(n + LX)
             ad(B + LL, 0)
             be(B, 1)
+            qh(n - LH)
+            qx(n + LX)
             ad(B + LL, 1)
             f2(n)
+            if 0 < n <= 12:
+                rA(n - 1)
             hst(n)
+
 
         def M2(t):
             M(t, 0)
@@ -387,52 +428,56 @@ def tile_loramlp_pa_t_kernel(tc, x, xa, W_gate_up, B_gate_up, A_down, out_0, out
 
         M2(28)
         M2(29)
-        HT(24)
-        HT(25)
+        HT(22)
+        HT(23)
         MX2(10)
         BE(28)
-        HTout(24, "S")
+        HTout(22, "S")
+        HTout(23, "S")
         c_(28)
         f_(28)
-        HTout(25, "S")
         HAout(10, "S")
         M2(30)
+        HT(24)
+        HT(25)
         BE(29)
         c_(29)
         f_(29)
         hst(14)
+        qh(11)
+        HTout(24, "S")
+        HTout(25, "S")
         M2(31)
-        HT(26)
-        HT(27)
         BE(30)
         c_(30)
-        HTout(26, "S")
+        HT(26)
+        HT(27)
         BE(31)
+        HTout(26, "S")
         c_(31)
+        MX2(11)
         HTout(27, "S")
         f_(30, "V")
         f_(31, "V")
         hst(15)
+        HAout(11, "S")
         HT(28)
         HT(29)
         HTout(28, "S")
         HTout(29, "S")
         HT(30)
         HT(31)
-        qh(11)
         qh(12)
+        qh(13)
         HTout(30, "S")
         HTout(31, "V")
-        MX2(11)
         MX2(12)
-        qh(13)
+        MX2(13)
         qh(14)
         qh(15)
-        HAout(11, "S")
         HAout(12, "S")
-        MX2(13)
+        HAout(13, "S")
         MX2(14)
         MX2(15)
-        HAout(13, "S")
         HAout(14, "V")
         HAout(15, "S")

@@ -151,19 +151,33 @@ def tile_loramlp_pa_t_kernel(tc, x, xa, W_gate_up, B_gate_up, A_down, out_0, out
                 if cc not in xaT:
                     XA(cc)
 
-        wg = const.tile([P, 2 * F, 4], BF16, name="wg", align_bytes=64)
+        wg = {}
 
-        def w_rg(hf):
-            nc.vector.tensor_copy(
-                out=wg[:, F * hf:F * hf + F, :].rearrange("p (c i) t -> p c t i", i=4),
-                in_=w_sb[hf][:].rearrange("p t (c i) -> p c t i", i=4),
-            )
+        def w_rg(hf, parts=1):
+            if hf == 0:
+                wg[hf] = const.tile([P, F, 4], BF16, name="wg0", align_bytes=64)
+                nc.vector.tensor_copy(
+                    out=wg[hf][:].rearrange("p (c i) t -> p c t i", i=4),
+                    in_=w_sb[hf][:].rearrange("p t (c i) -> p c t i", i=4),
+                )
+            else:
+                wg[hf] = const.tile([P, F, 4], BF16, tag="first", name="wg1", align_bytes=64)
+                w = F // parts
+                for k in range(parts):
+                    nc.gpsimd.tensor_scalar(
+                        out=wg[hf][:, w * k:w * k + w, :],
+                        in0=w_sb[hf][:, :, w * k:w * k + w].rearrange("p t c -> p c t"),
+                        scalar1=1.0,
+                        scalar2=0.0,
+                        op0=MULT,
+                        op1=ADD,
+                    )
 
         def w_q(hf):
             nc.vector.quantize_mx(
                 out=wc[:, F * hf:F * hf + F].bitcast(FP8X4),
                 scales=ws[:, F * hf:F * hf + F],
-                in_=wg[:, F * hf:F * hf + F, :].rearrange("p c t -> p (c t)"),
+                in_=wg[hf][:].rearrange("p c t -> p (c t)"),
             )
 
         def a_prep():
@@ -186,7 +200,10 @@ def tile_loramlp_pa_t_kernel(tc, x, xa, W_gate_up, B_gate_up, A_down, out_0, out
         def XTout(n, eng):
             if n < 0 or n >= NP:
                 return
-            xg[n] = work.tile([P, 2 * P * 4], BF16, tag="xg", name="xg", align_bytes=64)
+            if n == 0:
+                xg[n] = const.tile([P, 2 * P * 4], BF16, tag="first", name="xg0", align_bytes=64)
+            else:
+                xg[n] = work.tile([P, 2 * P * 4], BF16, tag="xg", name="xg", align_bytes=64)
             copy_on(
                 eng,
                 xg[n][:].bitcast(F32).rearrange("p (j t u) -> p j t u", j=2, u=2),
@@ -353,29 +370,53 @@ def tile_loramlp_pa_t_kernel(tc, x, xa, W_gate_up, B_gate_up, A_down, out_0, out
         ad(0, 0)
         ad(1, 0)
         w_rg(0)
-        L(2, 0)
-        ad(2, 0)
         XT(0)
         XTout(0, "S")
-        L(0, 1)
-        L(1, 1)
+        L(2, 0)
         w_q(0)
-        w_rg(1)
         qx(0)
+        w_rg(1)
+        ad(2, 0, "V")
+        L(0, 1)
         ad(0, 1)
+        L(1, 1)
         ad(1, 1)
         L(2, 1)
         ad(2, 1)
+        M(0, 0)
+        M(1, 0)
+        be(0, 0)
+        c_(0)
+        be(1, 0)
+        c_(1)
         XT(1)
-        XTout(1, "S")
-        w_q(1)
+        XTout(1, "V")
         L(3, 0)
-        L(3, 1)
-        need_xa(4)
         ad(3, 0)
+        need_xa(4)
+        L(3, 1)
         ad(3, 1)
+        XT(2)
+        XTout(2, "V")
+        L(4, 0)
+        ad(4, 0)
+        L(4, 1)
+        ad(4, 1)
+        w_q(1)
+        qx(1)
+        M(0, 1)
+        M(1, 1)
+        qx(2)
+        be(0, 1)
+        be(1, 1)
+        f2(0)
+        L(5, 0)
+        L(5, 1)
+        ad(5, 0)
+        ad(5, 1)
+        hst(0)
 
-        for n in range(NP - 2):
+        for n in range(1, NP - 2):
             A = 2 * n
             B = A + 1
             M(A, 0)
@@ -403,8 +444,6 @@ def tile_loramlp_pa_t_kernel(tc, x, xa, W_gate_up, B_gate_up, A_down, out_0, out
             L(B + LL, 1)
             c_(B)
             HAout(n - LH - 1, "V")
-            if n == 0:
-                qx(1)
             if n == 1:
                 a_prep()
             ad(B + LL, 0)
@@ -413,7 +452,7 @@ def tile_loramlp_pa_t_kernel(tc, x, xa, W_gate_up, B_gate_up, A_down, out_0, out
             qx(n + LX)
             ad(B + LL, 1)
             f2(n)
-            if 0 < n <= 12:
+            if 1 < n <= 12:
                 rA(n - 1)
             hst(n)
 

@@ -421,9 +421,9 @@ def tile_loramlp_pa_t_kernel(tc, x, xa, W_gate_up, B_gate_up, A_down, out_0, out
             B = A + 1
             M(A, 0)
             M(A, 1)
+            M(B, 0)
             L(A + LL, 0)
             L(A + LL, 1)
-            M(B, 0)
             be(A, 0)
             ad(A + LL, 0)
             be(A, 1)

@@ -434,13 +434,13 @@ def tile_loramlp_pa_t_kernel(tc, x, xa, W_gate_up, B_gate_up, A_down, out_0, out
                 need_xa(min(NT - 1, B + LL + 2))
             HT(2 * (n - LH))
             HT(2 * (n - LH) + 1)
+            L(B + LL, 0)
             MX2(n - LH - 1)
             be(B, 0)
             XTout(n + LX, "V" if n < 2 else "S")
             HTout(2 * (n - LH), "V")
             HTout(2 * (n - LH) + 1, "V")
             M(B, 1)
-            L(B + LL, 0)
             L(B + LL, 1)
             c_(B)
             HAout(n - LH - 1, "V")

from contextlib import ExitStack

import concourse.bass as bass
import concourse.mybir as mybir
import concourse.tile as tile
from concourse.masks import make_identity

F32 = mybir.dt.float32
BF16 = mybir.dt.bfloat16
U32 = mybir.dt.uint32
U8 = mybir.dt.uint8
FP8X4 = mybir.dt.float8_e4m3fn_x4
ADD = mybir.AluOpType.add
MULT = mybir.AluOpType.mult
SILU = mybir.ActivationFunctionType.Silu

T, D, F, R = 4096, 512, 512, 128
P = 128
NT = T // P
NP = NT // 2
FLOPS = 2 * T * D * 2 * F + 2 * T * R * 2 * F + 2 * T * F * R

PIN = True
LX = 2
LH = 3
LL = 4
LL0 = 3
XCH = 4
LS_BUFS = 12
TAIL_S = 0
HT2S = 0
HA_ENG = "S"


def tile_loramlp_pa_t_kernel(tc, x, xa, W_gate_up, B_gate_up, A_down, out_0, out_1):
    nc = tc.nc
    with ExitStack() as ctx:
        const = ctx.enter_context(tc.tile_pool(name="const", bufs=1))
        work = ctx.enter_context(tc.tile_pool(name="work", bufs=3))
        ps = ctx.enter_context(tc.psum_pool(name="ps", bufs=8))
        if PIN:
            ctx.enter_context(tc.manual_schedule())

        x_v = x.rearrange("(p i) d -> p i d", i=NT)
        xa_v = xa.rearrange("(p i) r -> p i r", i=NT)
        h_v = out_0.rearrange("(p i) f -> p i f", i=NT)
        ha_v = out_1.rearrange("(p i) r -> p i r", i=NT)

        zero = const.tile([P, 1], F32, name="zero")
        warm = const.tile([P, 1], F32, name="warm")
        nc.vector.memset(zero[:], 0.0)
        nc.scalar.activation(out=warm[:], in_=zero[:], func=SILU)
        ident_b = const.tile([P, P], BF16, name="ident_b")
        make_identity(nc, ident_b[:])
        ident_f = const.tile([P, P], F32, name="ident_f")
        make_identity(nc, ident_f[:])

        xa_chunks = [(0, 4), (4, 4), (8, 8), (16, 8), (24, 8)]
        xa_sb = [const.tile([P, cnt * R], BF16, name="xa_sb%d" % c) for c, (i0, cnt) in enumerate(xa_chunks)]
        xa_of = {}
        for c, (i0, cnt) in enumerate(xa_chunks):
            for k in range(cnt):
                xa_of[i0 + k] = (c, k)
        x_chunks = [(0, 2), (2, 2)] + [(i0, 4) for i0 in range(4, NT, 4)]
        x_sb = [const.tile([P, cnt * D], BF16, name="x_sb%d" % c) for c, (i0, cnt) in enumerate(x_chunks)]
        x_of = {}
        for c, (i0, cnt) in enumerate(x_chunks):
            for k in range(cnt):
                x_of[i0 + k] = (c, k)
        b_sb = [const.tile([P, F], BF16, name="b_sb%d" % hf) for hf in range(2)]
        w_sb = [const.tile([P, 4, F], BF16, name="w_sb%d" % hf) for hf in range(2)]
        a_sb = const.tile([P, 4, R], BF16, name="a_sb")

        def load_xa(c):
            i0, cnt = xa_chunks[c]
            nc.sync.dma_start(out=xa_sb[c][:].rearrange("p (i r) -> p i r", r=R), in_=xa_v[:, i0:i0 + cnt, :])

        def load_b(hf):
            nc.sync.dma_start(out=b_sb[hf][:], in_=B_gate_up[:, F * hf:F * hf + F])

        def load_x(c):
            i0, cnt = x_chunks[c]
            nc.sync.dma_start(out=x_sb[c][:].rearrange("p (i d) -> p i d", d=D), in_=x_v[:, i0:i0 + cnt, :])

        def load_w(hf):
            for u in range(2):
                nc.sync.dma_start(
                    out=w_sb[hf][:, 2 * u:2 * u + 2, :],
                    in_=W_gate_up[256 * u:256 * u + 256, F * hf:F * hf + F].rearrange("(q e) c -> q e c", e=2),
                )

        load_xa(0)
        load_b(0)
        load_w(0)
        load_x(0)
        load_b(1)
        load_w(1)
        load_x(1)
        load_xa(1)
        load_x(2)
        load_xa(2)
        load_x(3)
        nc.sync.dma_start(out=a_sb[:], in_=A_down.rearrange("(t p) n -> p t n", p=P))
        load_x(4)
        load_xa(3)
        load_x(5)
        load_x(6)
        load_xa(4)
        load_x(7)
        load_x(8)

        xaT = {}
        xt_ps = {}
        xg = {}
        xc = {}
        xs = {}
        l_ps = {}
        l_sb = {}
        m_ps = {}
        g_sb = {}
        u_sb = {}
        s_sb = {}
        h_sb = {}
        h16 = {}
        ht_ps = {}
        hg = {}
        hc = {}
        hs = {}
        ha_ps = {}
        wc = const.tile([P, 2 * F], U32, name="wc", align_bytes=64)
        ws = const.tile([P, 2 * F], U8, name="ws", align_bytes=64)
        ac = const.tile([P, R], U32, name="ac", align_bytes=64)
        asc = const.tile([P, R], U8, name="asc", align_bytes=64)

        def copy_on(eng, out, in_):
            if eng == "S":
                nc.scalar.copy(out=out, in_=in_)
            else:
                nc.vector.tensor_copy(out=out, in_=in_)

        def XA(c):
            cnt = xa_chunks[c][1]
            t = ps.tile([P, cnt, P], BF16, tag="ps", name="xat_ps")
            for j in range(cnt):
                nc.tensor.transpose(out=t[:, j, :], in_=xa_sb[c][:, R * j:R * j + R], identity=ident_b[:])
            xaT[c] = const.tile([P, cnt * P], BF16, name="xaT%d" % c)
            nc.scalar.copy(out=xaT[c][:], in_=t[:].rearrange("p j t -> p (j t)"))

        def need_xa(t):
            for cc in range(xa_of[t][0] + 1):
                if cc not in xaT:
                    XA(cc)

        wg = {}

        def w_rg(hf, parts=1):
            if hf == 0:
                wg[hf] = const.tile([P, F, 4], BF16, name="wg0", align_bytes=64)
                nc.vector.tensor_copy(
                    out=wg[hf][:].rearrange("p (c i) t -> p c t i", i=4),
                    in_=w_sb[hf][:].rearrange("p t (c i) -> p c t i", i=4),
                )
            else:
                wg[hf] = const.tile([P, F, 4], BF16, tag="first", name="wg1", align_bytes=64)
                w = F // parts
                for k in range(parts):
                    nc.gpsimd.tensor_scalar(
                        out=wg[hf][:, w * k:w * k + w, :],
                        in0=w_sb[hf][:, :, w * k:w * k + w].rearrange("p t c -> p c t"),
                        scalar1=1.0,
                        scalar2=0.0,
                        op0=MULT,
                        op1=ADD,
                    )

        def w_q(hf):
            nc.vector.quantize_mx(
                out=wc[:, F * hf:F * hf + F].bitcast(FP8X4),
                scales=ws[:, F * hf:F * hf + F],
                in_=wg[hf][:].rearrange("p c t -> p (c t)"),
            )

        def a_prep():
            ag = const.tile([P, R, 4], BF16, name="ag", align_bytes=64)
            nc.vector.tensor_copy(out=ag[:], in_=a_sb[:].rearrange("p t n -> p n t"))
            nc.vector.quantize_mx(out=ac[:].bitcast(FP8X4), scales=asc[:], in_=ag[:].rearrange("p n t -> p (n t)"))

        def XT(n):
            if n < 0 or n >= NP:
                return
            t = ps.tile([P, 2, 2, P], F32, tag="ps", name="xt_ps")
            xt_ps[n] = t
            for j in range(2):
                i = 2 * n + j
                xw = x_sb[x_of[i][0]][:].bitcast(F32)
                base = x_of[i][1] * (D // 2)
                for u in range(2):
                    nc.tensor.transpose(out=t[:, j, u, :], in_=xw[:, base + P * u:base + P * u + P], identity=ident_f[:])

        def XTout(n, eng):
            if n < 0 or n >= NP:
                return
            if n == 0:
                xg[n] = const.tile([P, 2 * P * 4], BF16, tag="first", name="xg0", align_bytes=64)
            else:
                xg[n] = work.tile([P, 2 * P * 4], BF16, tag="xg", name="xg", align_bytes=64)
            copy_on(
                eng,
                xg[n][:].bitcast(F32).rearrange("p (j t u) -> p j t u", j=2, u=2),
                xt_ps[n][:].rearrange("p j u t -> p j t u"),
            )

        def qx(n):
            if n < 0 or n >= NP:
                return
            xc[n] = const.tile([P, 2 * P], U32, name="xc%d" % n, align_bytes=64)
            xs[n] = const.tile([P, 2 * P], U8, name="xs%d" % n, align_bytes=64)
            nc.vector.quantize_mx(out=xc[n][:].bitcast(FP8X4), scales=xs[n][:], in_=xg[n][:])

        def L(t, hf):
            if t < 0 or t >= NT:
                return
            b = ps.tile([P, F], F32, tag="ps", name="l_ps")
            l_ps[(t, hf)] = b
            c, k = xa_of[t]
            nc.tensor.matmul(out=b[:], lhsT=xaT[c][:, P * k:P * k + P], rhs=b_sb[hf][:], start=True, stop=True)

        def ad(t, hf, eng="S"):
            if t < 0 or t >= NT:
                return
            l_sb[(t, hf)] = work.tile([P, F], F32, tag="ls", name="l_sb", bufs=LS_BUFS)
            copy_on(eng, l_sb[(t, hf)][:], l_ps[(t, hf)][:])

        def M(t, hf):
            if t < 0 or t >= NT:
                return
            b = ps.tile([P, F], F32, tag="ps", name="m_ps")
            m_ps[(t, hf)] = b
            n = t // 2
            j = t % 2
            nc.tensor.matmul_mx(
                out=b[:],
                lhsT=xc[n][:, P * j:P * j + P].bitcast(FP8X4),
                lhsT_scale=xs[n][:, P * j:P * j + P],
                rhs=wc[:, F * hf:F * hf + F].bitcast(FP8X4),
                rhs_scale=ws[:, F * hf:F * hf + F],
                start=True,
                stop=True,
            )

        def be(t, hf):
            if t < 0 or t >= NT:
                return
            n = t // 2
            j = t % 2
            if hf:
                if j == 0:
                    u_sb[n] = work.tile([P, 2 * F], F32, tag="u", name="u_sb", bufs=3)
                o = u_sb[n][:, F * j:F * j + F]
            else:
                g_sb[t] = work.tile([P, F], F32, tag="g", name="g_sb", bufs=4)
                o = g_sb[t][:]
            nc.vector.tensor_tensor(out=o, in0=m_ps[(t, hf)][:], in1=l_sb[(t, hf)][:], op=ADD)

        def c_(t):
            if t < 0 or t >= NT:
                return
            n = t // 2
            j = t % 2
            if j == 0:
                s_sb[n] = work.tile([P, 2 * F], F32, tag="s", name="s_sb", bufs=3)
            nc.scalar.activation(out=s_sb[n][:, F * j:F * j + F], in_=g_sb[t][:], func=SILU)

        def f_(t, eng="G"):
            if t < 0 or t >= NT:
                return
            n = t // 2
            j = t % 2
            if j == 0:
                h_sb[n] = work.tile([P, 2 * F], F32, tag="h", name="h_sb", bufs=6)
            cols = slice(F * j, F * j + F)
            if eng == "G":
                nc.gpsimd.tensor_tensor(out=h_sb[n][:, cols], in0=s_sb[n][:, cols], in1=u_sb[n][:, cols], op=MULT)
            else:
                nc.vector.tensor_tensor(out=h_sb[n][:, cols], in0=s_sb[n][:, cols], in1=u_sb[n][:, cols], op=MULT)

        def f2(n):
            h_sb[n] = work.tile([P, 2 * F], F32, tag="h", name="h_sb", bufs=6)
            nc.gpsimd.tensor_tensor(out=h_sb[n][:], in0=s_sb[n][:], in1=u_sb[n][:], op=MULT)

        def rA(n):
            h16[n] = work.tile([P, 2, P, 2], BF16, tag="h16", name="h16", bufs=4)
            nc.gpsimd.tensor_scalar(
                out=h16[n][:],
                in0=h_sb[n][:, 0:F].rearrange("p (u e c) -> p u c e", u=2, e=2),
                scalar1=1.0,
                scalar2=0.0,
                op0=MULT,
                op1=ADD,
            )

        def hst(n):
            nc.sync.dma_start(out=h_v[:, 2 * n:2 * n + 2, :], in_=h_sb[n][:].rearrange("p (i f) -> p i f", f=F))

        def HT(t):
            if t < 0 or t >= NT:
                return
            n = t // 2
            j = t % 2
            if n in h16 and j == 0:
                b = ps.tile([P, 2, P], F32, tag="ps", name="ht_ps")
                hw = h16[n][:].rearrange("p u c e -> p (u c e)").bitcast(F32)
                for u in range(2):
                    nc.tensor.transpose(out=b[:, u, :], in_=hw[:, P * u:P * u + P], identity=ident_f[:])
            else:
                b = ps.tile([P, 4, P], F32, tag="ps", name="ht_ps")
                for q in range(4):
                    nc.tensor.transpose(out=b[:, q, :], in_=h_sb[n][:, F * j + P * q:F * j + P * q + P], identity=ident_f[:])
            ht_ps[t] = b

        def HTout(t, eng):
            if t < 0 or t >= NT:
                return
            n = t // 2
            j = t % 2
            if j == 0:
                hg[n] = work.tile([P, 2, P, 4], BF16, tag="hg", name="hg", align_bytes=64, bufs=6)
            if n in h16 and j == 0:
                copy_on(
                    eng,
                    hg[n][:, 0, :, :].rearrange("p r k -> p (r k)").bitcast(F32).rearrange("p (r u) -> p r u", u=2),
                    ht_ps[t][:].rearrange("p u r -> p r u"),
                )
            else:
                copy_on(eng, hg[n][:, j, :, :], ht_ps[t][:].rearrange("p q r -> p r q"))

        def qh(n):
            if n < 0 or n >= NP:
                return
            hc[n] = work.tile([P, 2 * P], U32, tag="hc", name="hc", align_bytes=64)
            hs[n] = work.tile([P, 2 * P], U8, tag="hs", name="hs", align_bytes=64)
            nc.vector.quantize_mx(out=hc[n][:].bitcast(FP8X4), scales=hs[n][:], in_=hg[n][:].rearrange("p j r q -> p (j r q)"))

        def MX2(n):
            if n < 0 or n >= NP:
                return
            b = ps.tile([P, 2, R], F32, tag="ps", name="ha_ps")
            ha_ps[n] = b
            for j in range(2):
                nc.tensor.matmul_mx(
                    out=b[:, j, :],
                    lhsT=hc[n][:, P * j:P * j + P].bitcast(FP8X4),
                    lhsT_scale=hs[n][:, P * j:P * j + P],
                    rhs=ac[:].bitcast(FP8X4),
                    rhs_scale=asc[:],
                    start=True,
                    stop=True,
                )

        def HAout(n, eng):
            if n < 0 or n >= NP:
                return
            o = work.tile([P, 2, R], F32, tag="ha", name="ha_sb", bufs=6)
            copy_on(eng, o[:], ha_ps[n][:])
            nc.sync.dma_start(out=ha_v[:, 2 * n:2 * n + 2, :], in_=o[:])

        need_xa(0)
        L(0, 0)
        L(1, 0)
        ad(0, 0)
        ad(1, 0)
        w_rg(0)
        XT(0)
        XTout(0, "S")
        L(2, 0)
        w_q(0)
        qx(0)
        w_rg(1)
        ad(2, 0, "V")
        L(0, 1)
        ad(0, 1)
        L(1, 1)
        ad(1, 1)
        L(2, 1)
        ad(2, 1)
        M(0, 0)
        M(1, 0)
        be(0, 0)
        c_(0)
        be(1, 0)
        c_(1)
        XT(1)
        XTout(1, "V")
        L(3, 0)
        ad(3, 0)
        need_xa(4)
        L(3, 1)
        ad(3, 1)
        XT(2)
        XTout(2, "V")
        L(4, 0)
        ad(4, 0)
        L(4, 1)
        ad(4, 1)
        w_q(1)
        qx(1)
        M(0, 1)
        M(1, 1)
        qx(2)
        be(0, 1)
        be(1, 1)
        f2(0)
        L(5, 0)
        L(5, 1)
        ad(5, 0)
        ad(5, 1)
        hst(0)

        for n in range(1, NP - 2):
            A = 2 * n
            B = A + 1
            M(A, 0)
            M(A, 1)
            M(B, 0)
            L(A + LL, 0)
            L(A + LL, 1)
            be(A, 0)
            ad(A + LL, 0)
            be(A, 1)
            ad(A + LL, 1, "V" if n < 2 else "S")
            c_(A)
            XT(n + LX)
            if B + LL + 2 < NT + 2:
                need_xa(min(NT - 1, B + LL + 2))
            HT(2 * (n - LH))
            HT(2 * (n - LH) + 1)
            L(B + LL, 0)
            MX2(n - LH - 1)
            be(B, 0)
            XTout(n + LX, "V" if n < 2 else "S")
            HTout(2 * (n - LH), "V")
            HTout(2 * (n - LH) + 1, "V")
            M(B, 1)
            L(B + LL, 1)
            c_(B)
            HAout(n - LH - 1, "V")
            if n == 1:
                a_prep()
            ad(B + LL, 0)
            be(B, 1)
            qh(n - LH)
            qx(n + LX)
            ad(B + LL, 1)
            f2(n)
            if 1 < n <= 12:
                rA(n - 1)
            hst(n)


        def M2(t):
            M(t, 0)
            M(t, 1)

        def BE(t):
            be(t, 0)
            be(t, 1)

        M2(28)
        M2(29)
        HT(22)
        HT(23)
        MX2(10)
        BE(28)
        HTout(22, "S")
        HTout(23, "S")
        c_(28)
        f_(28)
        HAout(10, "S")
        M2(30)
        HT(24)
        HT(25)
        BE(29)
        c_(29)
        f_(29)
        hst(14)
        qh(11)
        HTout(24, "S")
        HTout(25, "S")
        M2(31)
        BE(30)
        c_(30)
        HT(26)
        HT(27)
        BE(31)
        HTout(26, "S")
        c_(31)
        MX2(11)
        HTout(27, "S")
        f_(30, "V")
        f_(31, "V")
        hst(15)
        HAout(11, "S")
        HT(28)
        HT(29)
        HTout(28, "S")
        HTout(29, "S")
        HT(30)
        HT(31)
        qh(12)
        qh(13)
        HTout(30, "S")
        HTout(31, "V")
        MX2(12)
        MX2(13)
        qh(14)
        qh(15)
        HAout(12, "S")
        HAout(13, "S")
        MX2(14)
        MX2(15)
        HAout(14, "V")
        HAout(15, "S")
